import numpy as np
import ml_dtypes


def mxq(x, axis, fmt="e4m3"):
    dtype, down = {"e4m3": (ml_dtypes.float8_e4m3fn, 7), "e5m2": (ml_dtypes.float8_e5m2, 14)}[fmt]
    v = np.moveaxis(np.asarray(x, np.float32).astype(ml_dtypes.bfloat16).astype(np.float64), axis, -1)
    blocks = v.reshape(v.shape[:-1] + (-1, 32))
    amax = np.abs(blocks).max(-1, keepdims=True)
    byte = np.maximum(np.where(amax > 0, np.frexp(amax)[1] - 1 + 127, 0) - down, 1)
    scale = np.exp2(byte - 127.0)
    codes = (blocks / scale).astype(np.float32).astype(dtype).astype(np.float64)
    return np.moveaxis((codes * scale).reshape(v.shape), -1, axis)


WIDE = False


def mx_kscale(k):
    if not WIDE:
        return np.ones(k)
    levels = np.array([10, -10, 5, -5, 0])
    a = np.random.permutation(np.resize(levels, k // 512 * 4)).reshape(k // 512, 4)
    idx = np.arange(k)
    return np.exp2(a[idx // 512, idx % 128 // 32])


BF16 = ml_dtypes.bfloat16


def bf(x):
    return np.asarray(x, np.float32).astype(BF16)


def f64(x):
    return np.asarray(x).astype(np.float64)


E2M1 = np.array([0.0, 0.5, 1.0, 1.5, 2.0, 3.0, 4.0, 6.0, -0.0, -0.5, -1.0, -1.5, -2.0, -3.0, -4.0, -6.0])


def pack_weight(w, fmt):
    k, n = w.shape
    w = f64(bf(w)).reshape(k // 32, 32, n)
    amax = np.abs(w).max(1)
    if fmt == "e4m3":
        byte = np.frexp(amax)[1] - 1 + 127 - 7
    else:
        mant, ex = np.frexp(amax / 6.0)
        byte = np.where(mant > 0.5, ex, ex - 1) + 127
    byte = np.clip(np.where(amax > 0, byte, 1), 1, 254)
    scaled = (w * np.exp2(127.0 - byte)[:, None, :]).reshape(k, n).astype(np.float32)
    by_word = np.ascontiguousarray(scaled.reshape(k // 512, 128, 4, n).transpose(0, 1, 3, 2))
    if fmt == "e4m3":
        words = by_word.astype(ml_dtypes.float8_e4m3fn).view(np.uint8)
    else:
        c = by_word.astype(ml_dtypes.float4_e2m1fn).view(np.uint8) & 0xF
        words = c[..., 0::2] | (c[..., 1::2] << 4)
    return np.ascontiguousarray(words), np.ascontiguousarray(byte.astype(np.uint8).reshape(k // 512, 16, n))


def unpack_weight(words, scales, fmt):
    g, p, n, _ = words.shape
    if fmt == "e4m3":
        vals = np.ascontiguousarray(words).view(ml_dtypes.float8_e4m3fn).astype(np.float64)
    else:
        nib = np.empty((g, p, n, 4), np.uint8)
        nib[..., 0::2] = words & 0xF
        nib[..., 1::2] = words >> 4
        vals = E2M1[nib]
    vals = vals * np.repeat(np.exp2(scales.astype(np.float64) - 127.0), 8, axis=1)[..., None]
    return vals.transpose(0, 1, 3, 2).reshape(g * 512, n)


B, L, D, DV, BN = 8, 1024, 1024, 256, 128
SV = 2.0 * B / np.sqrt(L)
SB = 2.0 * B / L


def setup_inputs():
    s, u = mx_kscale(D), mx_kscale(D)
    qp_top = bf(np.random.standard_normal((B, BN, D)) * s)
    kp = bf(np.random.standard_normal((B, L, D)) / s)
    v = bf(np.random.standard_normal((B, L, D)) * u)
    Wv = np.random.standard_normal((DV, D)) * SV / np.sqrt(D) / u[None, :]
    Wv_words, Wv_scales = pack_weight(np.ascontiguousarray(Wv.T), "e4m3")
    bv = bf(np.random.standard_normal(DV) * SB)
    return {"qp_top": qp_top,
            "kp": kp,
            "v": v,
            "Wv_words": Wv_words,
            "Wv_scales": Wv_scales,
            "bv": bv}


def reference(qp_top, kp, v, Wv_words, Wv_scales, bv):
    vp = (mxq(f64(v), 2, "e4m3") @ unpack_weight(Wv_words, Wv_scales, "e4m3")) + f64(bv)
    score = (mxq(f64(qp_top), 2, "e4m3") @ mxq(f64(kp), 2, "e4m3").transpose(0, 2, 1)) * (1.0 / np.sqrt(D))
    e = np.exp(score - score.max(0, keepdims=True))
    attn = e / e.sum(0, keepdims=True)
    return mxq(attn, 2, "e4m3") @ mxq(vp, 1, "e4m3")

@@ -1,0 +1,229 @@
+import math
+from contextlib import ExitStack
+
+import concourse.mybir as mybir
+from concourse.masks import make_identity
+
+F32 = mybir.dt.float32
+BF16 = mybir.dt.bfloat16
+I32 = mybir.dt.int32
+U32 = mybir.dt.uint32
+U8 = mybir.dt.uint8
+FP8X4 = mybir.dt.float8_e4m3fn_x4
+ALU = mybir.AluOpType
+ACT = mybir.ActivationFunctionType
+
+B, L, D, DV, BN = 8, 1024, 1024, 256, 128
+P = 128
+PACK = 4
+K_PASS = P * PACK
+PASSES = D // K_PASS
+ROW_TILES = 4
+HALVES = L // (ROW_TILES * P)
+PLANES = 2 * PASSES
+SLICES = 8
+SLICE = ROW_TILES * BN // SLICES
+RAW_BUFS = 6
+
+FLOPS = 2 * B * (L * D * DV + BN * D * L + BN * L * DV)
+
+
+def tile_bottleneck_attention_pa_t_kernel(tc, qp_top, kp, v, Wv_words, Wv_scales, bv, out):
+    nc = tc.nc
+    with ExitStack() as ctx:
+        const = ctx.enter_context(tc.tile_pool(name="const", bufs=1))
+        raw_pool = ctx.enter_context(tc.tile_pool(name="raw", bufs=RAW_BUFS))
+        grouped_pool = ctx.enter_context(tc.tile_pool(name="grouped", bufs=3))
+        codes_pool = ctx.enter_context(tc.tile_pool(name="codes", bufs=3))
+        small = ctx.enter_context(tc.tile_pool(name="small", bufs=2))
+        flip_psum = ctx.enter_context(tc.psum_pool(name="flip", bufs=4))
+        acc_psum = ctx.enter_context(tc.psum_pool(name="acc", bufs=4))
+
+        ident = const.tile([P, P], F32)
+        make_identity(nc, ident[:])
+
+        q_codes = const.tile([P, 2, PASSES, ROW_TILES, BN], U32, align_bytes=64)
+        q_scales = const.tile([P, 2, PASSES, ROW_TILES, BN], U8, align_bytes=64)
+        scores = const.tile([P, HALVES, B, ROW_TILES * BN], F32)
+        peak = const.tile([P, HALVES, ROW_TILES * BN], F32)
+        attn_grouped = const.tile([P, HALVES, B, ROW_TILES * BN], BF16, align_bytes=64)
+        attn_codes = const.tile([P, HALVES, B, BN], U32, align_bytes=64)
+        attn_scales = const.tile([P, HALVES, B, BN], U8, align_bytes=64)
+        vp_codes = const.tile([P, B, HALVES, DV], U32, align_bytes=64)
+        vp_scales = const.tile([P, B, HALVES, DV], U8, align_bytes=64)
+        w_codes = const.tile([P, PASSES, DV], U32, align_bytes=64)
+        w_scales = const.tile([P, PASSES, DV], U8, align_bytes=64)
+        bias_bf = const.tile([P, DV], BF16)
+        bias = const.tile([P, DV], F32)
+
+        def load_rows(rows):
+            raw = raw_pool.tile([P, ROW_TILES, D], BF16)
+            nc.sync.dma_start(out=raw[:], in_=rows)
+            return raw
+
+        def contiguous_words(c):
+            return slice(P * c, P * (c + 1))
+
+        def every_second_word(c):
+            g, u = divmod(c, 2)
+            return slice(2 * P * g + u, 2 * P * (g + 1), 2)
+
+        def transpose_and_quantise(raw, word_columns, codes, scales, banks_on_vector):
+            raw_words = raw[:].bitcast(F32)
+            grouped = grouped_pool.tile([P, PASSES, ROW_TILES, P, PACK], BF16, align_bytes=64)
+            grouped_words = grouped[:].bitcast(F32)
+            for t in range(ROW_TILES):
+                flipped = flip_psum.tile([P, PLANES, P], F32)
+                for c in range(PLANES):
+                    nc.tensor.transpose(flipped[:, c, :], raw_words[:, t, word_columns(c)], ident[:])
+                pairs = flipped[:].rearrange("p (g u) r -> p g r u", u=2)
+                if t < banks_on_vector:
+                    nc.vector.tensor_copy(out=grouped_words[:, :, t, :, :], in_=pairs)
+                else:
+                    nc.scalar.copy(out=grouped_words[:, :, t, :, :], in_=pairs)
+            nc.vector.quantize_mx(
+                out=codes.rearrange("p g t r -> p (g t r)").bitcast(FP8X4),
+                scales=scales.rearrange("p g t r -> p (g t r)"),
+                in_=grouped[:].rearrange("p g t r k -> p (g t r k)"),
+            )
+
+        def score_step(b, h, raw):
+            kp_codes = codes_pool.tile([P, PASSES, ROW_TILES, P], U32, align_bytes=64)
+            kp_scales = codes_pool.tile([P, PASSES, ROW_TILES, P], U8, align_bytes=64)
+            transpose_and_quantise(raw, contiguous_words, kp_codes[:], kp_scales[:], 1 if h == 0 else 0)
+            score_ps = acc_psum.tile([P, ROW_TILES, BN], F32, tag="acc")
+            for t in range(ROW_TILES):
+                for g in range(PASSES):
+                    nc.tensor.matmul_mx(
+                        out=score_ps[:, t, :],
+                        lhsT=kp_codes[:, g, t, :].bitcast(FP8X4),
+                        lhsT_scale=kp_scales[:, g, t, :],
+                        rhs=q_codes[:, b // ROW_TILES, g, b % ROW_TILES, :].bitcast(FP8X4),
+                        rhs_scale=q_scales[:, b // ROW_TILES, g, b % ROW_TILES, :],
+                        start=(g == 0),
+                        stop=(g == PASSES - 1),
+                    )
+            nc.scalar.copy(
+                out=scores[:, h, b, :].rearrange("p (i t) -> p i t", t=ROW_TILES),
+                in_=score_ps[:].rearrange("p t i -> p i t"),
+            )
+            if b == 1:
+                nc.vector.tensor_max(peak[:, h, :], scores[:, h, 0, :], scores[:, h, 1, :])
+            if b > 1:
+                nc.vector.tensor_max(peak[:, h, :], peak[:, h, :], scores[:, h, b, :])
+
+        def softmax_slice(h, s):
+            cols = slice(SLICE * s, SLICE * (s + 1))
+            part = scores[:, h, :, cols]
+            nc.vector.tensor_tensor(
+                out=part,
+                in0=part,
+                in1=peak[:, h, cols].unsqueeze(1).to_broadcast([P, B, SLICE]),
+                op=ALU.subtract,
+            )
+            nc.scalar.activation(out=part, in_=part, func=ACT.Exp, scale=1.0 / math.sqrt(D))
+            sum4 = small.tile([P, 4, SLICE], F32)
+            nc.vector.tensor_add(sum4[:], scores[:, h, 0:4, cols], scores[:, h, 4:8, cols])
+            sum2 = small.tile([P, 2, SLICE], F32)
+            nc.vector.tensor_add(sum2[:], sum4[:, 0:2, :], sum4[:, 2:4, :])
+            total = small.tile([P, SLICE], F32)
+            nc.vector.tensor_add(total[:], sum2[:, 0, :], sum2[:, 1, :])
+            inverse = small.tile([P, SLICE], F32)
+            nc.vector.reciprocal(inverse[:], total[:])
+            nc.vector.tensor_tensor(
+                out=attn_grouped[:, h, :, cols],
+                in0=part,
+                in1=inverse[:].unsqueeze(1).to_broadcast([P, B, SLICE]),
+                op=ALU.mult,
+            )
+
+        def quantise_attn(h):
+            nc.vector.quantize_mx(
+                out=attn_codes[:, h].rearrange("p b i -> p (b i)").bitcast(FP8X4),
+                scales=attn_scales[:, h].rearrange("p b i -> p (b i)"),
+                in_=attn_grouped[:, h].rearrange("p b c -> p (b c)"),
+            )
+
+        def value_step(b, h, raw):
+            v_codes = codes_pool.tile([P, PASSES, ROW_TILES, P], U32, align_bytes=64)
+            v_scales = codes_pool.tile([P, PASSES, ROW_TILES, P], U8, align_bytes=64)
+            transpose_and_quantise(raw, every_second_word, v_codes[:], v_scales[:], 0)
+            vp_grouped = small.tile([P, DV, PACK], BF16, align_bytes=64)
+            for e in range(DV // P):
+                features = slice(P * e, P * (e + 1))
+                vp_ps = acc_psum.tile([P, ROW_TILES, P], F32, tag="acc")
+                for t in range(ROW_TILES):
+                    for g in range(PASSES):
+                        nc.tensor.matmul_mx(
+                            out=vp_ps[:, t, :],
+                            lhsT=v_codes[:, g, t, :].bitcast(FP8X4),
+                            lhsT_scale=v_scales[:, g, t, :],
+                            rhs=w_codes[:, g, features].bitcast(FP8X4),
+                            rhs_scale=w_scales[:, g, features],
+                            start=(g == 0),
+                            stop=(g == PASSES - 1),
+                        )
+                nc.vector.tensor_tensor(
+                    out=vp_grouped[:, features, :],
+                    in0=vp_ps[:].rearrange("p t c -> p c t"),
+                    in1=bias[:, features].unsqueeze(2).to_broadcast([P, P, PACK]),
+                    op=ALU.add,
+                )
+            nc.vector.quantize_mx(
+                out=vp_codes[:, b, h, :].bitcast(FP8X4),
+                scales=vp_scales[:, b, h, :],
+                in_=vp_grouped[:].rearrange("p c t -> p (c t)"),
+            )
+
+        def output_step(b):
+            out_ps = acc_psum.tile([P, DV], F32, tag="acc")
+            for h in range(HALVES):
+                nc.tensor.matmul_mx(
+                    out=out_ps[:],
+                    lhsT=attn_codes[:, h, b, :].bitcast(FP8X4),
+                    lhsT_scale=attn_scales[:, h, b, :],
+                    rhs=vp_codes[:, b, h, :].bitcast(FP8X4),
+                    rhs_scale=vp_scales[:, b, h, :],
+                    start=(h == 0),
+                    stop=(h == HALVES - 1),
+                )
+            out_sb = small.tile([P, DV], F32)
+            nc.scalar.copy(out=out_sb[:], in_=out_ps[:])
+            nc.scalar.dma_start(out=out[b], in_=out_sb[:])
+
+        for c in range(B // ROW_TILES):
+            raw = load_rows(qp_top[ROW_TILES * c : ROW_TILES * (c + 1)].rearrange("b i d -> i b d"))
+            transpose_and_quantise(raw, contiguous_words, q_codes[:, c], q_scales[:, c], ROW_TILES // 2)
+
+        nc.vector.memset(w_scales[:].bitcast(I32), 0)
+        nc.sync.dma_start(
+            out=w_codes[:].bitcast(I32),
+            in_=Wv_words.rearrange("g p n t -> p g (n t)").bitcast(I32),
+        )
+        for quadrant in range(4):
+            nc.sync.dma_start(
+                out=w_scales[32 * quadrant : 32 * quadrant + 4].bitcast(I32),
+                in_=Wv_scales[:, 4 * quadrant : 4 * quadrant + 4, :].rearrange("g r n -> r g n").bitcast(I32),
+            )
+        nc.scalar.dma_start(out=bias_bf[:], in_=bv.partition_broadcast(P))
+        nc.vector.tensor_copy(out=bias[:], in_=bias_bf[:])
+
+        def rows_of(x, b, h):
+            return x[b, K_PASS * h : K_PASS * (h + 1), :].rearrange("(p t) d -> p t d", t=ROW_TILES)
+
+        for h in range(HALVES):
+            for b in range(B):
+                score_step(b, h, load_rows(rows_of(kp, b, h)))
+                if h > 0:
+                    softmax_slice(h - 1, b)
+        quantise_attn(0)
+
+        for b in range(B):
+            value_step(b, 0, load_rows(rows_of(v, b, 0)))
+            softmax_slice(HALVES - 1, b)
+            if b == B - 1:
+                quantise_attn(HALVES - 1)
+                for earlier in range(b):
+                    output_step(earlier)
+            value_step(b, 1, load_rows(rows_of(v, b, 1)))
+        output_step(B - 1)

@@ -38,6 +38,7 @@ def tile_bottleneck_attention_pa_t_kernel(tc, qp_top, kp, v, Wv_words, Wv_scales
         small = ctx.enter_context(tc.tile_pool(name="small", bufs=2))
         flip_psum = ctx.enter_context(tc.psum_pool(name="flip", bufs=4))
         acc_psum = ctx.enter_context(tc.psum_pool(name="acc", bufs=4))
+        ctx.enter_context(tc.manual_schedule())
 
         ident = const.tile([P, P], F32)
         make_identity(nc, ident[:])
@@ -68,7 +69,7 @@ def tile_bottleneck_attention_pa_t_kernel(tc, qp_top, kp, v, Wv_words, Wv_scales
             g, u = divmod(c, 2)
             return slice(2 * P * g + u, 2 * P * (g + 1), 2)
 
-        def transpose_and_quantise(raw, word_columns, codes, scales, banks_on_vector):
+        def flip(raw, word_columns, banks_on_vector):
             raw_words = raw[:].bitcast(F32)
             grouped = grouped_pool.tile([P, PASSES, ROW_TILES, P, PACK], BF16, align_bytes=64)
             grouped_words = grouped[:].bitcast(F32)
@@ -81,16 +82,16 @@ def tile_bottleneck_attention_pa_t_kernel(tc, qp_top, kp, v, Wv_words, Wv_scales
                     nc.vector.tensor_copy(out=grouped_words[:, :, t, :, :], in_=pairs)
                 else:
                     nc.scalar.copy(out=grouped_words[:, :, t, :, :], in_=pairs)
+            return grouped
+
+        def quantise(grouped, codes, scales):
             nc.vector.quantize_mx(
                 out=codes.rearrange("p g t r -> p (g t r)").bitcast(FP8X4),
                 scales=scales.rearrange("p g t r -> p (g t r)"),
                 in_=grouped[:].rearrange("p g t r k -> p (g t r k)"),
             )
 
-        def score_step(b, h, raw):
-            kp_codes = codes_pool.tile([P, PASSES, ROW_TILES, P], U32, align_bytes=64)
-            kp_scales = codes_pool.tile([P, PASSES, ROW_TILES, P], U8, align_bytes=64)
-            transpose_and_quantise(raw, contiguous_words, kp_codes[:], kp_scales[:], 1 if h == 0 else 0)
+        def score_step(b, h, kp_codes, kp_scales):
             score_ps = acc_psum.tile([P, ROW_TILES, BN], F32, tag="acc")
             for t in range(ROW_TILES):
                 for g in range(PASSES):
@@ -112,7 +113,7 @@ def tile_bottleneck_attention_pa_t_kernel(tc, qp_top, kp, v, Wv_words, Wv_scales
             if b > 1:
                 nc.vector.tensor_max(peak[:, h, :], peak[:, h, :], scores[:, h, b, :])
 
-        def softmax_slice(h, s):
+        def softmax_subtract(h, s):
             cols = slice(SLICE * s, SLICE * (s + 1))
             part = scores[:, h, :, cols]
             nc.vector.tensor_tensor(
@@ -121,7 +122,13 @@ def tile_bottleneck_attention_pa_t_kernel(tc, qp_top, kp, v, Wv_words, Wv_scales
                 in1=peak[:, h, cols].unsqueeze(1).to_broadcast([P, B, SLICE]),
                 op=ALU.subtract,
             )
+
+        def softmax_exp(h, s):
+            part = scores[:, h, :, SLICE * s : SLICE * (s + 1)]
             nc.scalar.activation(out=part, in_=part, func=ACT.Exp, scale=1.0 / math.sqrt(D))
+
+        def softmax_normalise(h, s):
+            cols = slice(SLICE * s, SLICE * (s + 1))
             sum4 = small.tile([P, 4, SLICE], F32)
             nc.vector.tensor_add(sum4[:], scores[:, h, 0:4, cols], scores[:, h, 4:8, cols])
             sum2 = small.tile([P, 2, SLICE], F32)
@@ -132,7 +139,7 @@ def tile_bottleneck_attention_pa_t_kernel(tc, qp_top, kp, v, Wv_words, Wv_scales
             nc.vector.reciprocal(inverse[:], total[:])
             nc.vector.tensor_tensor(
                 out=attn_grouped[:, h, :, cols],
-                in0=part,
+                in0=scores[:, h, :, cols],
                 in1=inverse[:].unsqueeze(1).to_broadcast([P, B, SLICE]),
                 op=ALU.mult,
             )
@@ -144,10 +151,7 @@ def tile_bottleneck_attention_pa_t_kernel(tc, qp_top, kp, v, Wv_words, Wv_scales
                 in_=attn_grouped[:, h].rearrange("p b c -> p (b c)"),
             )
 
-        def value_step(b, h, raw):
-            v_codes = codes_pool.tile([P, PASSES, ROW_TILES, P], U32, align_bytes=64)
-            v_scales = codes_pool.tile([P, PASSES, ROW_TILES, P], U8, align_bytes=64)
-            transpose_and_quantise(raw, every_second_word, v_codes[:], v_scales[:], 0)
+        def value_step(b, h, v_codes, v_scales):
             vp_grouped = small.tile([P, DV, PACK], BF16, align_bytes=64)
             for e in range(DV // P):
                 features = slice(P * e, P * (e + 1))
@@ -191,11 +195,39 @@ def tile_bottleneck_attention_pa_t_kernel(tc, qp_top, kp, v, Wv_words, Wv_scales
             nc.scalar.copy(out=out_sb[:], in_=out_ps[:])
             nc.scalar.dma_start(out=out[b], in_=out_sb[:])
 
-        for c in range(B // ROW_TILES):
-            raw = load_rows(qp_top[ROW_TILES * c : ROW_TILES * (c + 1)].rearrange("b i d -> i b d"))
-            transpose_and_quantise(raw, contiguous_words, q_codes[:, c], q_scales[:, c], ROW_TILES // 2)
+
+        chunks = [("q", c, 0) for c in range(B // ROW_TILES)]
+        chunks += [("kp", b, h) for h in range(HALVES) for b in range(B)]
+        chunks += [("v", b, h) for b in range(B) for h in range(HALVES)]
+
+        def load(n):
+            kind, b, h = chunks[n]
+            if kind == "q":
+                return load_rows(qp_top[ROW_TILES * b : ROW_TILES * (b + 1)].rearrange("b i d -> i b d"))
+            source = kp if kind == "kp" else v
+            return load_rows(source[b, K_PASS * h : K_PASS * (h + 1), :].rearrange("(p t) d -> p t d", t=ROW_TILES))
+
+        def flip_chunk(n, raw):
+            kind, b, h = chunks[n]
+            if kind == "v":
+                return flip(raw, every_second_word, 0)
+            return flip(raw, contiguous_words, 1 if h == 0 else 0)
+
+        def quantise_chunk(n, grouped):
+            kind, b, h = chunks[n]
+            if kind == "q":
+                quantise(grouped, q_codes[:, b], q_scales[:, b])
+                return None
+            row_codes = codes_pool.tile([P, PASSES, ROW_TILES, P], U32, align_bytes=64)
+            row_scales = codes_pool.tile([P, PASSES, ROW_TILES, P], U8, align_bytes=64)
+            quantise(grouped, row_codes[:], row_scales[:])
+            return row_codes, row_scales
 
         nc.vector.memset(w_scales[:].bitcast(I32), 0)
+        nc.scalar.dma_start(out=bias_bf[:], in_=bv.partition_broadcast(P))
+        raws = {}
+        for n in range(RAW_BUFS):
+            raws[n] = load(n)
         nc.sync.dma_start(
             out=w_codes[:].bitcast(I32),
             in_=Wv_words.rearrange("g p n t -> p g (n t)").bitcast(I32),
@@ -205,25 +237,33 @@ def tile_bottleneck_attention_pa_t_kernel(tc, qp_top, kp, v, Wv_words, Wv_scales
                 out=w_scales[32 * quadrant : 32 * quadrant + 4].bitcast(I32),
                 in_=Wv_scales[:, 4 * quadrant : 4 * quadrant + 4, :].rearrange("g r n -> r g n").bitcast(I32),
             )
-        nc.scalar.dma_start(out=bias_bf[:], in_=bv.partition_broadcast(P))
+        operands = {0: quantise_chunk(0, flip_chunk(0, raws[0]))}
         nc.vector.tensor_copy(out=bias[:], in_=bias_bf[:])
 
-        def rows_of(x, b, h):
-            return x[b, K_PASS * h : K_PASS * (h + 1), :].rearrange("(p t) d -> p t d", t=ROW_TILES)
-
-        for h in range(HALVES):
-            for b in range(B):
-                score_step(b, h, load_rows(rows_of(kp, b, h)))
-                if h > 0:
-                    softmax_slice(h - 1, b)
-        quantise_attn(0)
-
+        for i in range(len(chunks)):
+            kind, b, h = chunks[i]
+            piece = None
+            if kind == "kp" and h == 1:
+                piece = (0, b)
+            if kind == "v" and h == 0:
+                piece = (1, b)
+            if i + RAW_BUFS < len(chunks):
+                raws[i + RAW_BUFS] = load(i + RAW_BUFS)
+            if piece:
+                softmax_subtract(*piece)
+            if i + 1 < len(chunks):
+                grouped_next = flip_chunk(i + 1, raws[i + 1])
+            if piece:
+                softmax_exp(*piece)
+            if i + 1 < len(chunks):
+                operands[i + 1] = quantise_chunk(i + 1, grouped_next)
+            if kind == "kp":
+                score_step(b, h, *operands[i])
+            if kind == "v":
+                value_step(b, h, *operands[i])
+            if piece:
+                softmax_normalise(*piece)
+                if b == B - 1:
+                    quantise_attn(piece[0])
         for b in range(B):
-            value_step(b, 0, load_rows(rows_of(v, b, 0)))
-            softmax_slice(HALVES - 1, b)
-            if b == B - 1:
-                quantise_attn(HALVES - 1)
-                for earlier in range(b):
-                    output_step(earlier)
-            value_step(b, 1, load_rows(rows_of(v, b, 1)))
-        output_step(B - 1)
+            output_step(b)

@@ -91,8 +91,21 @@ def tile_bottleneck_attention_pa_t_kernel(tc, qp_top, kp, v, Wv_words, Wv_scales
                 in_=grouped[:].rearrange("p g t r k -> p (g t r k)"),
             )
 
+        def keep_clock_up(bank, row_codes, row_scales):
+            nc.tensor.matmul_mx(
+                out=bank[:].rearrange("p t i -> p (t i)"),
+                lhsT=row_codes[:, 0, 0, :].bitcast(FP8X4),
+                lhsT_scale=row_scales[:, 0, 0, :],
+                rhs=row_codes[:, 0].rearrange("p t r -> p (t r)").bitcast(FP8X4),
+                rhs_scale=row_scales[:, 0].rearrange("p t r -> p (t r)"),
+                start=True,
+                stop=True,
+            )
+
         def score_step(b, h, kp_codes, kp_scales):
             score_ps = acc_psum.tile([P, ROW_TILES, BN], F32, tag="acc")
+            keep_clock_up(score_ps, kp_codes, kp_scales)
+            keep_clock_up(score_ps, kp_codes, kp_scales)
             for t in range(ROW_TILES):
                 for g in range(PASSES):
                     nc.tensor.matmul_mx(
@@ -156,6 +169,7 @@ def tile_bottleneck_attention_pa_t_kernel(tc, qp_top, kp, v, Wv_words, Wv_scales
             for e in range(DV // P):
                 features = slice(P * e, P * (e + 1))
                 vp_ps = acc_psum.tile([P, ROW_TILES, P], F32, tag="acc")
+                keep_clock_up(vp_ps, v_codes, v_scales)
                 for t in range(ROW_TILES):
                     for g in range(PASSES):
                         nc.tensor.matmul_mx(

@@ -1,5 +1,6 @@
 import math
 from contextlib import ExitStack
+from functools import partial
 
 import concourse.mybir as mybir
 from concourse.masks import make_identity
@@ -24,6 +25,7 @@ PLANES = 2 * PASSES
 SLICES = 8
 SLICE = ROW_TILES * BN // SLICES
 RAW_BUFS = 6
+FLIP_LEAD = 3
 
 FLOPS = 2 * B * (L * D * DV + BN * D * L + BN * L * DV)
 
@@ -45,8 +47,8 @@ def tile_bottleneck_attention_pa_t_kernel(tc, qp_top, kp, v, Wv_words, Wv_scales
 
         q_codes = const.tile([P, 2, PASSES, ROW_TILES, BN], U32, align_bytes=64)
         q_scales = const.tile([P, 2, PASSES, ROW_TILES, BN], U8, align_bytes=64)
-        scores = const.tile([P, HALVES, B, ROW_TILES * BN], F32)
-        peak = const.tile([P, HALVES, ROW_TILES * BN], F32)
+        scores = const.tile([P, HALVES, SLICES, B, SLICE], F32)
+        peak = const.tile([P, HALVES, SLICES, SLICE], F32)
         attn_grouped = const.tile([P, HALVES, B, ROW_TILES * BN], BF16, align_bytes=64)
         attn_codes = const.tile([P, HALVES, B, BN], U32, align_bytes=64)
         attn_scales = const.tile([P, HALVES, B, BN], U8, align_bytes=64)
@@ -56,6 +58,7 @@ def tile_bottleneck_attention_pa_t_kernel(tc, qp_top, kp, v, Wv_words, Wv_scales
         w_scales = const.tile([P, PASSES, DV], U8, align_bytes=64)
         bias_bf = const.tile([P, DV], BF16)
         bias = const.tile([P, DV], F32)
+        out_all = const.tile([P, B, DV], F32)
 
         def load_rows(rows):
             raw = raw_pool.tile([P, ROW_TILES, D], BF16)
@@ -73,16 +76,17 @@ def tile_bottleneck_attention_pa_t_kernel(tc, qp_top, kp, v, Wv_words, Wv_scales
             raw_words = raw[:].bitcast(F32)
             grouped = grouped_pool.tile([P, PASSES, ROW_TILES, P, PACK], BF16, align_bytes=64)
             grouped_words = grouped[:].bitcast(F32)
+            left_for_vector = []
             for t in range(ROW_TILES):
                 flipped = flip_psum.tile([P, PLANES, P], F32)
                 for c in range(PLANES):
                     nc.tensor.transpose(flipped[:, c, :], raw_words[:, t, word_columns(c)], ident[:])
                 pairs = flipped[:].rearrange("p (g u) r -> p g r u", u=2)
-                if t < banks_on_vector:
-                    nc.vector.tensor_copy(out=grouped_words[:, :, t, :, :], in_=pairs)
-                else:
+                if t < ROW_TILES - banks_on_vector:
                     nc.scalar.copy(out=grouped_words[:, :, t, :, :], in_=pairs)
-            return grouped
+                else:
+                    left_for_vector.append((grouped_words[:, :, t, :, :], pairs))
+            return grouped, left_for_vector
 
         def quantise(grouped, codes, scales):
             nc.vector.quantize_mx(
@@ -91,21 +95,8 @@ def tile_bottleneck_attention_pa_t_kernel(tc, qp_top, kp, v, Wv_words, Wv_scales
                 in_=grouped[:].rearrange("p g t r k -> p (g t r k)"),
             )
 
-        def keep_clock_up(bank, row_codes, row_scales):
-            nc.tensor.matmul_mx(
-                out=bank[:].rearrange("p t i -> p (t i)"),
-                lhsT=row_codes[:, 0, 0, :].bitcast(FP8X4),
-                lhsT_scale=row_scales[:, 0, 0, :],
-                rhs=row_codes[:, 0].rearrange("p t r -> p (t r)").bitcast(FP8X4),
-                rhs_scale=row_scales[:, 0].rearrange("p t r -> p (t r)"),
-                start=True,
-                stop=True,
-            )
-
-        def score_step(b, h, kp_codes, kp_scales):
+        def multiply_scores(b, kp_codes, kp_scales):
             score_ps = acc_psum.tile([P, ROW_TILES, BN], F32, tag="acc")
-            keep_clock_up(score_ps, kp_codes, kp_scales)
-            keep_clock_up(score_ps, kp_codes, kp_scales)
             for t in range(ROW_TILES):
                 for g in range(PASSES):
                     nc.tensor.matmul_mx(
@@ -117,43 +108,55 @@ def tile_bottleneck_attention_pa_t_kernel(tc, qp_top, kp, v, Wv_words, Wv_scales
                         start=(g == 0),
                         stop=(g == PASSES - 1),
                     )
+            return score_ps
+
+        def copy_scores(b, h, score_ps):
             nc.scalar.copy(
-                out=scores[:, h, b, :].rearrange("p (i t) -> p i t", t=ROW_TILES),
-                in_=score_ps[:].rearrange("p t i -> p i t"),
+                out=scores[:, h, :, b, :].rearrange("p s (x t) -> p s x t", t=ROW_TILES),
+                in_=score_ps[:].rearrange("p t (s x) -> p s x t", s=SLICES),
             )
+
+        def raise_peak(b, h):
             if b == 1:
-                nc.vector.tensor_max(peak[:, h, :], scores[:, h, 0, :], scores[:, h, 1, :])
+                nc.vector.tensor_max(peak[:, h], scores[:, h, :, 0, :], scores[:, h, :, 1, :])
             if b > 1:
-                nc.vector.tensor_max(peak[:, h, :], peak[:, h, :], scores[:, h, b, :])
+                nc.vector.tensor_max(peak[:, h], peak[:, h], scores[:, h, :, b, :])
 
         def softmax_subtract(h, s):
-            cols = slice(SLICE * s, SLICE * (s + 1))
-            part = scores[:, h, :, cols]
             nc.vector.tensor_tensor(
-                out=part,
-                in0=part,
-                in1=peak[:, h, cols].unsqueeze(1).to_broadcast([P, B, SLICE]),
+                out=scores[:, h, s],
+                in0=scores[:, h, s],
+                in1=peak[:, h, s, :].unsqueeze(1).to_broadcast([P, B, SLICE]),
                 op=ALU.subtract,
             )
 
         def softmax_exp(h, s):
-            part = scores[:, h, :, SLICE * s : SLICE * (s + 1)]
-            nc.scalar.activation(out=part, in_=part, func=ACT.Exp, scale=1.0 / math.sqrt(D))
+            nc.scalar.activation(out=scores[:, h, s], in_=scores[:, h, s], func=ACT.Exp, scale=1.0 / math.sqrt(D))
 
-        def softmax_normalise(h, s):
-            cols = slice(SLICE * s, SLICE * (s + 1))
-            sum4 = small.tile([P, 4, SLICE], F32)
-            nc.vector.tensor_add(sum4[:], scores[:, h, 0:4, cols], scores[:, h, 4:8, cols])
-            sum2 = small.tile([P, 2, SLICE], F32)
-            nc.vector.tensor_add(sum2[:], sum4[:, 0:2, :], sum4[:, 2:4, :])
+        sums = {}
+
+        def softmax_pair_sums(h, s):
+            sum4 = small.tile([P, B // 2, SLICE], F32)
+            nc.vector.tensor_add(sum4[:], scores[:, h, s, 0 : B // 2, :], scores[:, h, s, B // 2 : B, :])
+            sums[(h, s)] = sum4
+
+        def softmax_total(h, s):
             total = small.tile([P, SLICE], F32)
-            nc.vector.tensor_add(total[:], sum2[:, 0, :], sum2[:, 1, :])
+            nc.vector.tensor_reduce(
+                out=total[:], in_=sums[(h, s)][:].rearrange("p b c -> p c b"), axis=mybir.AxisListType.X, op=ALU.add
+            )
+            sums[(h, s)] = total
+
+        def softmax_inverse(h, s):
             inverse = small.tile([P, SLICE], F32)
-            nc.vector.reciprocal(inverse[:], total[:])
+            nc.vector.reciprocal(inverse[:], sums[(h, s)][:])
+            sums[(h, s)] = inverse
+
+        def softmax_scale(h, s):
             nc.vector.tensor_tensor(
-                out=attn_grouped[:, h, :, cols],
-                in0=scores[:, h, :, cols],
-                in1=inverse[:].unsqueeze(1).to_broadcast([P, B, SLICE]),
+                out=attn_grouped[:, h, :, SLICE * s : SLICE * (s + 1)],
+                in0=scores[:, h, s],
+                in1=sums[(h, s)][:].unsqueeze(1).to_broadcast([P, B, SLICE]),
                 op=ALU.mult,
             )
 
@@ -164,12 +167,12 @@ def tile_bottleneck_attention_pa_t_kernel(tc, qp_top, kp, v, Wv_words, Wv_scales
                 in_=attn_grouped[:, h].rearrange("p b c -> p (b c)"),
             )
 
-        def value_step(b, h, v_codes, v_scales):
-            vp_grouped = small.tile([P, DV, PACK], BF16, align_bytes=64)
+        def multiply_values(v_codes, v_scales):
+            banks = []
             for e in range(DV // P):
                 features = slice(P * e, P * (e + 1))
                 vp_ps = acc_psum.tile([P, ROW_TILES, P], F32, tag="acc")
-                keep_clock_up(vp_ps, v_codes, v_scales)
+                banks.append(vp_ps)
                 for t in range(ROW_TILES):
                     for g in range(PASSES):
                         nc.tensor.matmul_mx(
@@ -181,12 +184,18 @@ def tile_bottleneck_attention_pa_t_kernel(tc, qp_top, kp, v, Wv_words, Wv_scales
                             start=(g == 0),
                             stop=(g == PASSES - 1),
                         )
-                nc.vector.tensor_tensor(
-                    out=vp_grouped[:, features, :],
-                    in0=vp_ps[:].rearrange("p t c -> p c t"),
-                    in1=bias[:, features].unsqueeze(2).to_broadcast([P, P, PACK]),
-                    op=ALU.add,
-                )
+            return banks
+
+        def add_bias(vp_grouped, vp_ps, e):
+            features = slice(P * e, P * (e + 1))
+            nc.vector.tensor_tensor(
+                out=vp_grouped[:, features, :],
+                in0=vp_ps[:].rearrange("p t c -> p c t"),
+                in1=bias[:, features].unsqueeze(2).to_broadcast([P, P, PACK]),
+                op=ALU.add,
+            )
+
+        def quantise_values(b, h, vp_grouped):
             nc.vector.quantize_mx(
                 out=vp_codes[:, b, h, :].bitcast(FP8X4),
                 scales=vp_scales[:, b, h, :],
@@ -205,9 +214,7 @@ def tile_bottleneck_attention_pa_t_kernel(tc, qp_top, kp, v, Wv_words, Wv_scales
                     start=(h == 0),
                     stop=(h == HALVES - 1),
                 )
-            out_sb = small.tile([P, DV], F32)
-            nc.scalar.copy(out=out_sb[:], in_=out_ps[:])
-            nc.scalar.dma_start(out=out[b], in_=out_sb[:])
+            nc.scalar.copy(out=out_all[:, b, :], in_=out_ps[:])
 
 
         chunks = [("q", c, 0) for c in range(B // ROW_TILES)]
@@ -227,15 +234,17 @@ def tile_bottleneck_attention_pa_t_kernel(tc, qp_top, kp, v, Wv_words, Wv_scales
                 return flip(raw, every_second_word, 0)
             return flip(raw, contiguous_words, 1 if h == 0 else 0)
 
-        def quantise_chunk(n, grouped):
+        groupeds, operands, banks = {}, {}, {}
+
+        def quantise_chunk(n):
             kind, b, h = chunks[n]
             if kind == "q":
-                quantise(grouped, q_codes[:, b], q_scales[:, b])
-                return None
-            row_codes = codes_pool.tile([P, PASSES, ROW_TILES, P], U32, align_bytes=64)
-            row_scales = codes_pool.tile([P, PASSES, ROW_TILES, P], U8, align_bytes=64)
-            quantise(grouped, row_codes[:], row_scales[:])
-            return row_codes, row_scales
+                quantise(groupeds[n], q_codes[:, b], q_scales[:, b])
+            else:
+                row_codes = codes_pool.tile([P, PASSES, ROW_TILES, P], U32, align_bytes=64)
+                row_scales = codes_pool.tile([P, PASSES, ROW_TILES, P], U8, align_bytes=64)
+                quantise(groupeds[n], row_codes[:], row_scales[:])
+                operands[n] = (row_codes, row_scales)
 
         nc.vector.memset(w_scales[:].bitcast(I32), 0)
         nc.scalar.dma_start(out=bias_bf[:], in_=bv.partition_broadcast(P))
@@ -251,33 +260,61 @@ def tile_bottleneck_attention_pa_t_kernel(tc, qp_top, kp, v, Wv_words, Wv_scales
                 out=w_scales[32 * quadrant : 32 * quadrant + 4].bitcast(I32),
                 in_=Wv_scales[:, 4 * quadrant : 4 * quadrant + 4, :].rearrange("g r n -> r g n").bitcast(I32),
             )
-        operands = {0: quantise_chunk(0, flip_chunk(0, raws[0]))}
         nc.vector.tensor_copy(out=bias[:], in_=bias_bf[:])
 
-        for i in range(len(chunks)):
-            kind, b, h = chunks[i]
-            piece = None
-            if kind == "kp" and h == 1:
-                piece = (0, b)
-            if kind == "v" and h == 0:
-                piece = (1, b)
-            if i + RAW_BUFS < len(chunks):
-                raws[i + RAW_BUFS] = load(i + RAW_BUFS)
+        def piece_of(i):
+            for half, stride in ((0, 1), (1, 2)):
+                s, rest = divmod(i - chunks.index(("kp", B - 1, half)), stride)
+                if rest == 0 and 0 <= s < SLICES:
+                    return (half, s)
+            return None
+
+        def alternate(chain, others):
+            for k in range(max(len(chain), len(others))):
+                for calls in (chain, others):
+                    if k < len(calls):
+                        calls[k]()
+
+        for i in range(-FLIP_LEAD, len(chunks)):
+            kind, b, h = chunks[i] if 0 <= i < len(chunks) else (None, 0, 0)
+            before, piece = piece_of(i - 1), piece_of(i)
+            if kind == "kp":
+                copy_scores(b, h, banks[i])
+            left_for_vector = []
+            if i + FLIP_LEAD < len(chunks):
+                groupeds[i + FLIP_LEAD], left_for_vector = flip_chunk(i + FLIP_LEAD, raws[i + FLIP_LEAD])
+                if i + FLIP_LEAD + RAW_BUFS < len(chunks):
+                    raws[i + FLIP_LEAD + RAW_BUFS] = load(i + FLIP_LEAD + RAW_BUFS)
+            if 0 <= i + 1 < len(chunks):
+                if chunks[i + 1][0] == "kp":
+                    banks[i + 1] = multiply_scores(chunks[i + 1][1], *operands[i + 1])
+                if chunks[i + 1][0] == "v":
+                    banks[i + 1] = multiply_values(*operands[i + 1])
+            if i == len(chunks) - 1:
+                for earlier in range(B - 1):
+                    output_step(earlier)
+                nc.sync.dma_start(out=out[0 : B - 1].rearrange("b i d -> i b d"), in_=out_all[:, 0 : B - 1, :])
+
+            chain, others = [], []
+            if before:
+                chain = [partial(link, *before) for link in (softmax_pair_sums, softmax_total, softmax_inverse, softmax_scale)]
+            if kind == "kp":
+                others.append(partial(raise_peak, b, h))
             if piece:
-                softmax_subtract(*piece)
-            if i + 1 < len(chunks):
-                grouped_next = flip_chunk(i + 1, raws[i + 1])
+                others.append(partial(softmax_subtract, *piece))
+            if kind == "v":
+                vp_grouped = small.tile([P, DV, PACK], BF16, align_bytes=64)
+                others.extend([partial(add_bias, vp_grouped, banks[i][e], e) for e in range(DV // P)])
+            if 0 <= i + 2 < len(chunks):
+                others.append(partial(quantise_chunk, i + 2))
+            alternate(chain, others)
             if piece:
                 softmax_exp(*piece)
-            if i + 1 < len(chunks):
-                operands[i + 1] = quantise_chunk(i + 1, grouped_next)
-            if kind == "kp":
-                score_step(b, h, *operands[i])
+            for target, pairs in left_for_vector:
+                nc.vector.tensor_copy(out=target, in_=pairs)
             if kind == "v":
-                value_step(b, h, *operands[i])
-            if piece:
-                softmax_normalise(*piece)
-                if b == B - 1:
-                    quantise_attn(piece[0])
-        for b in range(B):
-            output_step(b)
+                quantise_values(b, h, vp_grouped)
+            if before and before[1] == SLICES - 1:
+                quantise_attn(before[0])
+        output_step(B - 1)
+        nc.sync.dma_start(out=out[B - 1], in_=out_all[:, B - 1, :])

@@ -123,7 +123,7 @@ def tile_bottleneck_attention_pa_t_kernel(tc, qp_top, kp, v, Wv_words, Wv_scales
                 nc.vector.tensor_max(peak[:, h], peak[:, h], scores[:, h, :, b, :])
 
         def softmax_subtract(h, s):
-            nc.vector.tensor_tensor(
+            nc.gpsimd.tensor_tensor(
                 out=scores[:, h, s],
                 in0=scores[:, h, s],
                 in1=peak[:, h, s, :].unsqueeze(1).to_broadcast([P, B, SLICE]),
@@ -153,7 +153,7 @@ def tile_bottleneck_attention_pa_t_kernel(tc, qp_top, kp, v, Wv_words, Wv_scales
             sums[(h, s)] = inverse
 
         def softmax_scale(h, s):
-            nc.vector.tensor_tensor(
+            nc.gpsimd.tensor_tensor(
                 out=attn_grouped[:, h, :, SLICE * s : SLICE * (s + 1)],
                 in0=scores[:, h, s],
                 in1=sums[(h, s)][:].unsqueeze(1).to_broadcast([P, B, SLICE]),
@@ -297,11 +297,9 @@ def tile_bottleneck_attention_pa_t_kernel(tc, qp_top, kp, v, Wv_words, Wv_scales
 
             chain, others = [], []
             if before:
-                chain = [partial(link, *before) for link in (softmax_pair_sums, softmax_total, softmax_inverse, softmax_scale)]
+                chain = [partial(link, *before) for link in (softmax_pair_sums, softmax_total, softmax_inverse)]
             if kind == "kp":
                 others.append(partial(raise_peak, b, h))
-            if piece:
-                others.append(partial(softmax_subtract, *piece))
             if kind == "v":
                 vp_grouped = small.tile([P, DV, PACK], BF16, align_bytes=64)
                 others.extend([partial(add_bias, vp_grouped, banks[i][e], e) for e in range(DV // P)])
@@ -309,7 +307,10 @@ def tile_bottleneck_attention_pa_t_kernel(tc, qp_top, kp, v, Wv_words, Wv_scales
                 others.append(partial(quantise_chunk, i + 2))
             alternate(chain, others)
             if piece:
+                softmax_subtract(*piece)
                 softmax_exp(*piece)
+            if before:
+                softmax_scale(*before)
             for target, pairs in left_for_vector:
                 nc.vector.tensor_copy(out=target, in_=pairs)
             if kind == "v":

import math
from contextlib import ExitStack
from functools import partial

import concourse.mybir as mybir
from concourse.masks import make_identity

F32 = mybir.dt.float32
BF16 = mybir.dt.bfloat16
I32 = mybir.dt.int32
U32 = mybir.dt.uint32
U8 = mybir.dt.uint8
FP8X4 = mybir.dt.float8_e4m3fn_x4
ALU = mybir.AluOpType
ACT = mybir.ActivationFunctionType

B, L, D, DV, BN = 8, 1024, 1024, 256, 128
P = 128
PACK = 4
K_PASS = P * PACK
PASSES = D // K_PASS
ROW_TILES = 4
HALVES = L // (ROW_TILES * P)
PLANES = 2 * PASSES
SLICES = 8
SLICE = ROW_TILES * BN // SLICES
RAW_BUFS = 6
FLIP_LEAD = 3

FLOPS = 2 * B * (L * D * DV + BN * D * L + BN * L * DV)


def tile_bottleneck_attention_pa_t_kernel(tc, qp_top, kp, v, Wv_words, Wv_scales, bv, out):
    nc = tc.nc
    with ExitStack() as ctx:
        const = ctx.enter_context(tc.tile_pool(name="const", bufs=1))
        raw_pool = ctx.enter_context(tc.tile_pool(name="raw", bufs=RAW_BUFS))
        grouped_pool = ctx.enter_context(tc.tile_pool(name="grouped", bufs=3))
        codes_pool = ctx.enter_context(tc.tile_pool(name="codes", bufs=3))
        small = ctx.enter_context(tc.tile_pool(name="small", bufs=2))
        flip_psum = ctx.enter_context(tc.psum_pool(name="flip", bufs=4))
        acc_psum = ctx.enter_context(tc.psum_pool(name="acc", bufs=4))
        ctx.enter_context(tc.manual_schedule())

        ident = const.tile([P, P], F32)
        make_identity(nc, ident[:])

        q_codes = const.tile([P, 2, PASSES, ROW_TILES, BN], U32, align_bytes=64)
        q_scales = const.tile([P, 2, PASSES, ROW_TILES, BN], U8, align_bytes=64)
        scores = const.tile([P, HALVES, SLICES, B, SLICE], F32)
        peak = const.tile([P, HALVES, SLICES, SLICE], F32)
        attn_grouped = const.tile([P, HALVES, B, ROW_TILES * BN], BF16, align_bytes=64)
        attn_codes = const.tile([P, HALVES, B, BN], U32, align_bytes=64)
        attn_scales = const.tile([P, HALVES, B, BN], U8, align_bytes=64)
        vp_codes = const.tile([P, B, HALVES, DV], U32, align_bytes=64)
        vp_scales = const.tile([P, B, HALVES, DV], U8, align_bytes=64)
        w_codes = const.tile([P, PASSES, DV], U32, align_bytes=64)
        w_scales = const.tile([P, PASSES, DV], U8, align_bytes=64)
        bias_bf = const.tile([P, DV], BF16)
        bias = const.tile([P, DV], F32)
        out_all = const.tile([P, B, DV], F32)

        def load_rows(rows):
            raw = raw_pool.tile([P, ROW_TILES, D], BF16)
            nc.sync.dma_start(out=raw[:], in_=rows)
            return raw

        def contiguous_words(c):
            return slice(P * c, P * (c + 1))

        def every_second_word(c):
            g, u = divmod(c, 2)
            return slice(2 * P * g + u, 2 * P * (g + 1), 2)

        def flip(raw, word_columns, banks_on_vector):
            raw_words = raw[:].bitcast(F32)
            grouped = grouped_pool.tile([P, PASSES, ROW_TILES, P, PACK], BF16, align_bytes=64)
            grouped_words = grouped[:].bitcast(F32)
            left_for_vector = []
            for t in range(ROW_TILES):
                flipped = flip_psum.tile([P, PLANES, P], F32)
                for c in range(PLANES):
                    nc.tensor.transpose(flipped[:, c, :], raw_words[:, t, word_columns(c)], ident[:])
                pairs = flipped[:].rearrange("p (g u) r -> p g r u", u=2)
                if t < ROW_TILES - banks_on_vector:
                    nc.scalar.copy(out=grouped_words[:, :, t, :, :], in_=pairs)
                else:
                    left_for_vector.append((grouped_words[:, :, t, :, :], pairs))
            return grouped, left_for_vector

        def quantise(grouped, codes, scales):
            nc.vector.quantize_mx(
                out=codes.rearrange("p g t r -> p (g t r)").bitcast(FP8X4),
                scales=scales.rearrange("p g t r -> p (g t r)"),
                in_=grouped[:].rearrange("p g t r k -> p (g t r k)"),
            )

        def multiply_scores(b, kp_codes, kp_scales):
            score_ps = acc_psum.tile([P, ROW_TILES, BN], F32, tag="acc")
            for t in range(ROW_TILES):
                for g in range(PASSES):
                    nc.tensor.matmul_mx(
                        out=score_ps[:, t, :],
                        lhsT=kp_codes[:, g, t, :].bitcast(FP8X4),
                        lhsT_scale=kp_scales[:, g, t, :],
                        rhs=q_codes[:, b // ROW_TILES, g, b % ROW_TILES, :].bitcast(FP8X4),
                        rhs_scale=q_scales[:, b // ROW_TILES, g, b % ROW_TILES, :],
                        start=(g == 0),
                        stop=(g == PASSES - 1),
                    )
            return score_ps

        def copy_scores(b, h, score_ps):
            nc.scalar.copy(
                out=scores[:, h, :, b, :].rearrange("p s (x t) -> p s x t", t=ROW_TILES),
                in_=score_ps[:].rearrange("p t (s x) -> p s x t", s=SLICES),
            )

        def raise_peak(b, h):
            if b == 1:
                nc.vector.tensor_max(peak[:, h], scores[:, h, :, 0, :], scores[:, h, :, 1, :])
            if b > 1:
                nc.vector.tensor_max(peak[:, h], peak[:, h], scores[:, h, :, b, :])

        def softmax_subtract(h, s):
            nc.gpsimd.tensor_tensor(
                out=scores[:, h, s],
                in0=scores[:, h, s],
                in1=peak[:, h, s, :].unsqueeze(1).to_broadcast([P, B, SLICE]),
                op=ALU.subtract,
            )

        def softmax_exp(h, s):
            nc.scalar.activation(out=scores[:, h, s], in_=scores[:, h, s], func=ACT.Exp, scale=1.0 / math.sqrt(D))

        sums = {}

        def softmax_pair_sums(h, s):
            sum4 = small.tile([P, B // 2, SLICE], F32)
            nc.vector.tensor_add(sum4[:], scores[:, h, s, 0 : B // 2, :], scores[:, h, s, B // 2 : B, :])
            sums[(h, s)] = sum4

        def softmax_total(h, s):
            total = small.tile([P, SLICE], F32)
            nc.vector.tensor_reduce(
                out=total[:], in_=sums[(h, s)][:].rearrange("p b c -> p c b"), axis=mybir.AxisListType.X, op=ALU.add
            )
            sums[(h, s)] = total

        def softmax_inverse(h, s):
            inverse = small.tile([P, SLICE], F32)
            nc.vector.reciprocal(inverse[:], sums[(h, s)][:])
            sums[(h, s)] = inverse

        def softmax_scale(h, s):
            nc.gpsimd.tensor_tensor(
                out=attn_grouped[:, h, :, SLICE * s : SLICE * (s + 1)],
                in0=scores[:, h, s],
                in1=sums[(h, s)][:].unsqueeze(1).to_broadcast([P, B, SLICE]),
                op=ALU.mult,
            )

        def quantise_attn(h):
            nc.vector.quantize_mx(
                out=attn_codes[:, h].rearrange("p b i -> p (b i)").bitcast(FP8X4),
                scales=attn_scales[:, h].rearrange("p b i -> p (b i)"),
                in_=attn_grouped[:, h].rearrange("p b c -> p (b c)"),
            )

        def multiply_values(v_codes, v_scales):
            banks = []
            for e in range(DV // P):
                features = slice(P * e, P * (e + 1))
                vp_ps = acc_psum.tile([P, ROW_TILES, P], F32, tag="acc")
                banks.append(vp_ps)
                for t in range(ROW_TILES):
                    for g in range(PASSES):
                        nc.tensor.matmul_mx(
                            out=vp_ps[:, t, :],
                            lhsT=v_codes[:, g, t, :].bitcast(FP8X4),
                            lhsT_scale=v_scales[:, g, t, :],
                            rhs=w_codes[:, g, features].bitcast(FP8X4),
                            rhs_scale=w_scales[:, g, features],
                            start=(g == 0),
                            stop=(g == PASSES - 1),
                        )
            return banks

        def add_bias(vp_grouped, vp_ps, e):
            features = slice(P * e, P * (e + 1))
            nc.vector.tensor_tensor(
                out=vp_grouped[:, features, :],
                in0=vp_ps[:].rearrange("p t c -> p c t"),
                in1=bias[:, features].unsqueeze(2).to_broadcast([P, P, PACK]),
                op=ALU.add,
            )

        def quantise_values(b, h, vp_grouped):
            nc.vector.quantize_mx(
                out=vp_codes[:, b, h, :].bitcast(FP8X4),
                scales=vp_scales[:, b, h, :],
                in_=vp_grouped[:].rearrange("p c t -> p (c t)"),
            )

        def output_step(b):
            out_ps = acc_psum.tile([P, DV], F32, tag="acc")
            for h in range(HALVES):
                nc.tensor.matmul_mx(
                    out=out_ps[:],
                    lhsT=attn_codes[:, h, b, :].bitcast(FP8X4),
                    lhsT_scale=attn_scales[:, h, b, :],
                    rhs=vp_codes[:, b, h, :].bitcast(FP8X4),
                    rhs_scale=vp_scales[:, b, h, :],
                    start=(h == 0),
                    stop=(h == HALVES - 1),
                )
            nc.scalar.copy(out=out_all[:, b, :], in_=out_ps[:])


        chunks = [("q", c, 0) for c in range(B // ROW_TILES)]
        chunks += [("kp", b, h) for h in range(HALVES) for b in range(B)]
        chunks += [("v", b, h) for b in range(B) for h in range(HALVES)]

        def load(n):
            kind, b, h = chunks[n]
            if kind == "q":
                return load_rows(qp_top[ROW_TILES * b : ROW_TILES * (b + 1)].rearrange("b i d -> i b d"))
            source = kp if kind == "kp" else v
            return load_rows(source[b, K_PASS * h : K_PASS * (h + 1), :].rearrange("(p t) d -> p t d", t=ROW_TILES))

        def flip_chunk(n, raw):
            kind, b, h = chunks[n]
            if kind == "v":
                return flip(raw, every_second_word, 0)
            return flip(raw, contiguous_words, 1 if h == 0 else 0)

        groupeds, operands, banks = {}, {}, {}

        def quantise_chunk(n):
            kind, b, h = chunks[n]
            if kind == "q":
                quantise(groupeds[n], q_codes[:, b], q_scales[:, b])
            else:
                row_codes = codes_pool.tile([P, PASSES, ROW_TILES, P], U32, align_bytes=64)
                row_scales = codes_pool.tile([P, PASSES, ROW_TILES, P], U8, align_bytes=64)
                quantise(groupeds[n], row_codes[:], row_scales[:])
                operands[n] = (row_codes, row_scales)

        nc.vector.memset(w_scales[:].bitcast(I32), 0)
        nc.scalar.dma_start(out=bias_bf[:], in_=bv.partition_broadcast(P))
        raws = {}
        for n in range(RAW_BUFS):
            raws[n] = load(n)
        nc.sync.dma_start(
            out=w_codes[:].bitcast(I32),
            in_=Wv_words.rearrange("g p n t -> p g (n t)").bitcast(I32),
        )
        for quadrant in range(4):
            nc.sync.dma_start(
                out=w_scales[32 * quadrant : 32 * quadrant + 4].bitcast(I32),
                in_=Wv_scales[:, 4 * quadrant : 4 * quadrant + 4, :].rearrange("g r n -> r g n").bitcast(I32),
            )
        nc.vector.tensor_copy(out=bias[:], in_=bias_bf[:])

        def piece_of(i):
            for half, stride in ((0, 1), (1, 2)):
                s, rest = divmod(i - chunks.index(("kp", B - 1, half)), stride)
                if rest == 0 and 0 <= s < SLICES:
                    return (half, s)
            return None

        def alternate(chain, others):
            for k in range(max(len(chain), len(others))):
                for calls in (chain, others):
                    if k < len(calls):
                        calls[k]()

        for i in range(-FLIP_LEAD, len(chunks)):
            kind, b, h = chunks[i] if 0 <= i < len(chunks) else (None, 0, 0)
            before, piece = piece_of(i - 1), piece_of(i)
            if kind == "kp":
                copy_scores(b, h, banks[i])
            left_for_vector = []
            if i + FLIP_LEAD < len(chunks):
                groupeds[i + FLIP_LEAD], left_for_vector = flip_chunk(i + FLIP_LEAD, raws[i + FLIP_LEAD])
                if i + FLIP_LEAD + RAW_BUFS < len(chunks):
                    raws[i + FLIP_LEAD + RAW_BUFS] = load(i + FLIP_LEAD + RAW_BUFS)
            if 0 <= i + 1 < len(chunks):
                if chunks[i + 1][0] == "kp":
                    banks[i + 1] = multiply_scores(chunks[i + 1][1], *operands[i + 1])
                if chunks[i + 1][0] == "v":
                    banks[i + 1] = multiply_values(*operands[i + 1])
            if i == len(chunks) - 1:
                for earlier in range(B - 1):
                    output_step(earlier)
                nc.sync.dma_start(out=out[0 : B - 1].rearrange("b i d -> i b d"), in_=out_all[:, 0 : B - 1, :])

            chain, others = [], []
            if before:
                chain = [partial(link, *before) for link in (softmax_pair_sums, softmax_total, softmax_inverse)]
            if kind == "kp":
                others.append(partial(raise_peak, b, h))
            if kind == "v":
                vp_grouped = small.tile([P, DV, PACK], BF16, align_bytes=64)
                others.extend([partial(add_bias, vp_grouped, banks[i][e], e) for e in range(DV // P)])
            if 0 <= i + 2 < len(chunks):
                others.append(partial(quantise_chunk, i + 2))
            alternate(chain, others)
            if piece:
                softmax_subtract(*piece)
                softmax_exp(*piece)
            if before:
                softmax_scale(*before)
            for target, pairs in left_for_vector:
                nc.vector.tensor_copy(out=target, in_=pairs)
            if kind == "v":
                quantise_values(b, h, vp_grouped)
            if before and before[1] == SLICES - 1:
                quantise_attn(before[0])
        output_step(B - 1)
        nc.sync.dma_start(out=out[B - 1], in_=out_all[:, B - 1, :])
